import numpy as np
import ml_dtypes


def mxq(x, axis, fmt="e4m3"):
    dtype, down = {"e4m3": (ml_dtypes.float8_e4m3fn, 7), "e5m2": (ml_dtypes.float8_e5m2, 14)}[fmt]
    v = np.moveaxis(np.asarray(x, np.float32).astype(ml_dtypes.bfloat16).astype(np.float64), axis, -1)
    blocks = v.reshape(v.shape[:-1] + (-1, 32))
    amax = np.abs(blocks).max(-1, keepdims=True)
    byte = np.maximum(np.where(amax > 0, np.frexp(amax)[1] - 1 + 127, 0) - down, 1)
    scale = np.exp2(byte - 127.0)
    codes = (blocks / scale).astype(np.float32).astype(dtype).astype(np.float64)
    return np.moveaxis((codes * scale).reshape(v.shape), -1, axis)


WIDE = False


def mx_kscale(k):
    if not WIDE:
        return np.ones(k)
    levels = np.array([10, -10, 5, -5, 0])
    if k % 512:
        return np.exp2(np.random.permutation(np.resize(levels, k // 32))).repeat(32)
    a = np.empty((k // 512, 16))
    for p in range(k // 512):
        a[p, :8] = np.random.permutation(np.resize(levels, 8))
        for g in range(8):
            far = levels[np.abs(levels - a[p, g]) >= 10]
            a[p, g + 8] = far[np.random.randint(len(far))]
    return np.exp2(a.ravel()).repeat(32)


BF16 = ml_dtypes.bfloat16


def bf(x):
    return np.asarray(x, np.float32).astype(BF16)


def f64(x):
    return np.asarray(x).astype(np.float64)


E2M1 = np.array([0.0, 0.5, 1.0, 1.5, 2.0, 3.0, 4.0, 6.0, -0.0, -0.5, -1.0, -1.5, -2.0, -3.0, -4.0, -6.0])


def pack_weight(w, fmt):
    k, n = w.shape
    w = f64(bf(w)).reshape(k // 32, 32, n)
    amax = np.abs(w).max(1)
    if fmt == "e4m3":
        byte = np.frexp(amax)[1] - 1 + 127 - 7
    else:
        mant, ex = np.frexp(amax / 6.0)
        byte = np.where(mant > 0.5, ex, ex - 1) + 127
    byte = np.clip(np.where(amax > 0, byte, 1), 1, 254)
    scaled = (w * np.exp2(127.0 - byte)[:, None, :]).reshape(k, n).astype(np.float32)
    by_word = np.ascontiguousarray(scaled.reshape(k // 512, 128, 4, n).transpose(0, 1, 3, 2))
    if fmt == "e4m3":
        words = by_word.astype(ml_dtypes.float8_e4m3fn).view(np.uint8)
    else:
        c = by_word.astype(ml_dtypes.float4_e2m1fn).view(np.uint8) & 0xF
        words = c[..., 0::2] | (c[..., 1::2] << 4)
    return np.ascontiguousarray(words), np.ascontiguousarray(byte.astype(np.uint8).reshape(k // 512, 16, n))


def unpack_weight(words, scales, fmt):
    g, p, n, _ = words.shape
    if fmt == "e4m3":
        vals = np.ascontiguousarray(words).view(ml_dtypes.float8_e4m3fn).astype(np.float64)
    else:
        nib = np.empty((g, p, n, 4), np.uint8)
        nib[..., 0::2] = words & 0xF
        nib[..., 1::2] = words >> 4
        vals = E2M1[nib]
    vals = vals * np.repeat(np.exp2(scales.astype(np.float64) - 127.0), 8, axis=1)[..., None]
    return vals.transpose(0, 1, 3, 2).reshape(g * 512, n)


B, T, C, H, D, R = 4, 1024, 1024, 4, 128, 512
EPS = 1e-6
THETA = 10000.0


def rmsnorm(v, w):
    var = np.mean(v * v, axis=-1, keepdims=True)
    return v * (1.0 / np.sqrt(var + EPS)) * w


def rope(v, cos, sin):
    re, im = v[..., 0::2], v[..., 1::2]
    c, s = cos[None, :, None, :], sin[None, :, None, :]
    return np.stack([re * c - im * s, re * s + im * c], axis=-1).reshape(v.shape)


def draw0():
    s, t = mx_kscale(C), mx_kscale(R)
    ang = np.outer(np.arange(T), 1.0 / THETA ** (np.arange(0, D, 2) / D))
    x = bf(np.random.standard_normal((B, T, C)) * s)
    w_kv_down = np.random.standard_normal((R, C)) / np.sqrt(C) / s[None, :] * t[:, None]
    w_kv_down_words, w_kv_down_scales = pack_weight(w_kv_down.T, "e4m3")
    w_kv_up = np.random.standard_normal((2 * H * D, R)) / np.sqrt(R) / t[None, :]
    w_kv_up_words, w_kv_up_scales = pack_weight(w_kv_up.T, "e4m3")
    return {"x": x,
            "w_kv_down_words": w_kv_down_words, "w_kv_down_scales": w_kv_down_scales,
            "w_kv_up_words": w_kv_up_words, "w_kv_up_scales": w_kv_up_scales,
            "k_norm_w": bf(1.0 + 0.1 * np.random.standard_normal(D)),
            "freqs_cos": bf(np.cos(ang)), "freqs_sin": bf(np.sin(ang))}


def core(x, w_kv_down_words, w_kv_down_scales, w_kv_up_words, w_kv_up_scales, k_norm_w, freqs_cos, freqs_sin):
    latent = mxq(f64(x), 2, "e4m3") @ unpack_weight(w_kv_down_words, w_kv_down_scales, "e4m3")
    kv = (mxq(latent, 2, "e4m3") @ unpack_weight(w_kv_up_words, w_kv_up_scales, "e4m3")).reshape(B, T, 2, H, D)
    xk, xv = kv[:, :, 0], kv[:, :, 1]
    return rope(rmsnorm(xk, f64(k_norm_w)), f64(freqs_cos), f64(freqs_sin)), xv


def e4m3fn_bytes(y):
    return np.clip(np.asarray(y, np.float64), -448.0, 448.0).astype(np.float32).astype(ml_dtypes.float8_e4m3fn).view(np.uint8)


def e4m3fn_values(b):
    return np.asarray(b, np.uint8).view(ml_dtypes.float8_e4m3fn).astype(np.float64)


def setup_inputs():
    d = draw0()
    x0 = np.asarray(d['x']).astype(np.float64)
    s = (np.max(np.abs(x0), axis=(0, 1), keepdims=True) / 448.0).astype(np.float32)
    out = {}
    for k, v in d.items():
        if k == 'x':
            out['x_bytes'] = e4m3fn_bytes(x0 / s.astype(np.float64))
            out['x_scale'] = s
        else:
            out[k] = v
    return out


def reference(x_bytes, x_scale, w_kv_down_words, w_kv_down_scales, w_kv_up_words, w_kv_up_scales, k_norm_w, freqs_cos, freqs_sin):
    return core(e4m3fn_values(x_bytes) * x_scale.astype(np.float64), w_kv_down_words, w_kv_down_scales, w_kv_up_words, w_kv_up_scales, k_norm_w, freqs_cos, freqs_sin)

@@ -1,0 +1,299 @@
+from contextlib import ExitStack
+
+import concourse.mybir as mybir
+from concourse.masks import make_identity
+
+B, T, C, H, D, R = 4, 1024, 1024, 4, 128, 512
+EPS = 1e-6
+FLOPS = 2 * B * T * C * R + 2 * B * T * R * 2 * H * D
+
+F32 = mybir.dt.float32
+BF16 = mybir.dt.bfloat16
+I32 = mybir.dt.int32
+U32 = mybir.dt.uint32
+U8 = mybir.dt.uint8
+FP8 = mybir.dt.float8_e4m3fn
+FP8X4 = mybir.dt.float8_e4m3fn_x4
+ACT = mybir.ActivationFunctionType
+ALU = mybir.AluOpType
+
+P = 128
+PACK = 4
+IT = T // P
+NT = B * IT
+HD = H * D
+G = C // (P * PACK)
+
+
+def tile_mla_pa_t_w8_kernel(
+    tc, x_bytes, x_scale, wd_words, wd_scales, wu_words, wu_scales, k_norm_w, f_cos, f_sin, out_k, out_v
+):
+    nc = tc.nc
+    with ExitStack() as ctx:
+        keep = ctx.enter_context(tc.tile_pool(name="keep", bufs=1))
+        work = ctx.enter_context(tc.tile_pool(name="work", bufs=3))
+        store = ctx.enter_context(tc.tile_pool(name="store", bufs=3))
+        psum = ctx.enter_context(tc.psum_pool(name="psum", bufs=2))
+        ctx.enter_context(tc.manual_schedule())
+
+        warm = keep.tile([P, 1], F32, name="warm")
+        nc.vector.memset(warm[:], 1.0)
+        nc.scalar.activation(out=warm[:], in_=warm[:], func=ACT.Sqrt)
+
+        loads = [(0, 0, 1), (0, 1, 1), (0, 2, 2), (0, 4, 4)]
+        loads += [(b, i, 4) for b in range(1, B) for i in (0, 4)]
+        bytes_of = {}
+
+        def load_x(entry):
+            b, i0, n = entry
+            xb = keep.tile([P, n, C], U8, name="xbytes_%d_%d" % (b, i0))
+            nc.sync.dma_start(out=xb[:], in_=x_bytes[b].rearrange("(p i) k -> p i k", i=IT)[:, i0 : i0 + n, :])
+            for i in range(n):
+                bytes_of[b * IT + i0 + i] = (xb, i)
+
+        load_x(loads[0])
+        wds_raw = keep.tile([P, G, R], U8, name="wds_raw", align_bytes=64)
+        wus = keep.tile([P, 2 * HD], U8, name="wus", align_bytes=64)
+        nc.vector.memset(wds_raw[:].bitcast(I32), 0)
+        nc.vector.memset(wus[:].bitcast(I32), 0)
+        for q in range(4):
+            nc.sync.dma_start(
+                out=wds_raw[32 * q : 32 * q + 4, :, :].bitcast(I32),
+                in_=wd_scales[:, 4 * q : 4 * q + 4, :].rearrange("g q n -> q g n").bitcast(I32),
+            )
+        wd_raw = keep.tile([P, G * R], I32, name="wd_raw", align_bytes=64)
+        for g in range(G):
+            nc.sync.dma_start(
+                out=wd_raw[:, g * R : (g + 1) * R], in_=wd_words[g].rearrange("p n t -> p (n t)").bitcast(I32)
+            )
+        load_x(loads[1])
+        for q in range(4):
+            nc.sync.dma_start(
+                out=wus[32 * q : 32 * q + 4, :].bitcast(I32), in_=wu_scales[0, 4 * q : 4 * q + 4, :].bitcast(I32)
+            )
+        load_x(loads[2])
+        wu = keep.tile([P, 2 * HD], I32, name="wu", align_bytes=64)
+        nc.sync.dma_start(out=wu[:], in_=wu_words[0].rearrange("p n t -> p (n t)").bitcast(I32))
+        for entry in loads[3:]:
+            load_x(entry)
+
+        xs = keep.tile([P, G * PACK], F32, name="xs")
+        nc.scalar.dma_start(
+            out=xs[:].rearrange("p (g t) -> p g t", t=PACK),
+            in_=x_scale.rearrange("a b (g p t) -> p (a b g) t", g=G, t=PACK),
+        )
+        cos_t = keep.tile([P, IT, D // 2], BF16, name="cos_t")
+        sin_t = keep.tile([P, IT, D // 2], BF16, name="sin_t")
+        gain = keep.tile([P, D], BF16, name="gain")
+        nc.scalar.dma_start(out=cos_t[:], in_=f_cos.rearrange("(p i) j -> p i j", i=IT))
+        nc.scalar.dma_start(out=sin_t[:], in_=f_sin.rearrange("(p i) j -> p i j", i=IT))
+        nc.scalar.dma_start(out=gain[:], in_=k_norm_w.partition_broadcast(P))
+
+        ident = keep.tile([P, P], F32, name="ident")
+        make_identity(nc, ident[:])
+
+        wd = keep.tile([P, G * R], I32, name="wd", align_bytes=64)
+        st = {}
+        wds = keep.tile([P, G, R], U8, name="wds", align_bytes=64)
+        for t in range(PACK):
+            eng = nc.gpsimd if t < 2 else nc.vector
+            eng.tensor_copy(out=wds[:, :, t * P : (t + 1) * P], in_=wds_raw[:, :, t::PACK])
+        for g in range(G):
+            nc.vector.tensor_copy(
+                out=wd[:, g * R : (g + 1) * R].rearrange("p (t m) -> p t m", t=PACK),
+                in_=wd_raw[:, g * R : (g + 1) * R].rearrange("p (m t) -> p t m", t=PACK),
+            )
+
+        gain_x = keep.tile([P, D], F32, name="gain_x")
+        ta = keep.tile([P, IT, D], F32, name="ta")
+        tb = keep.tile([P, IT, D], F32, name="tb")
+        gv = gain[:].rearrange("p (j e) -> p j e", e=2)
+        gx = gain_x[:].rearrange("p (j e) -> p j e", e=2)
+        nc.gpsimd.tensor_scalar(out=gx[:, :, 0:1], in0=gv[:, :, 1:2], scalar1=-1.0, scalar2=0.0, op0=ALU.mult, op1=ALU.add)
+        nc.gpsimd.tensor_copy(out=gx[:, :, 1:2], in_=gv[:, :, 0:1])
+        for tab, trig, w in ((ta, cos_t, gv), (tb, sin_t, gx)):
+            nc.gpsimd.tensor_tensor(
+                out=tab[:].rearrange("p i (j e) -> p i j e", e=2),
+                in0=trig[:].unsqueeze(3).to_broadcast([P, IT, D // 2, 2]),
+                in1=w.unsqueeze(1).to_broadcast([P, IT, D // 2, 2]),
+                op=ALU.mult,
+            )
+
+
+        def cast(n):
+            xb, i = bytes_of[n]
+            xw = work.tile([P, C], BF16, name="xw")
+            if n == 0:
+                nc.vector.tensor_copy(out=xw[:, : C // 2], in_=xb[:, i, : C // 2].bitcast(FP8))
+                nc.scalar.copy(out=xw[:, C // 2 :], in_=xb[:, i, C // 2 :].bitcast(FP8))
+            else:
+                nc.scalar.copy(out=xw[:], in_=xb[:, i, :].bitcast(FP8))
+            st["xw", n] = xw
+
+        def turn(n):
+            words = st.pop(("xw", n))[:].bitcast(F32)
+            xt = psum.tile([P, 2 * G, P], F32, name="xt")
+            for g in range(G):
+                for u in range(2):
+                    nc.tensor.transpose(xt[:, 2 * g + u, :], words[:, 256 * g + u : 256 * (g + 1) : 2], ident[:])
+            st["xt", n] = xt
+
+        def scale(n):
+            xt = st.pop(("xt", n))
+            xv = xt[:].rearrange("p a n -> p (a n)").bitcast(BF16)
+            xg = work.tile([P, G * 512], BF16, name="xg", align_bytes=64)
+            nc.vector.tensor_tensor(
+                out=xg[:].rearrange("p (g n u e) -> p n g u e", g=G, u=2, e=2),
+                in0=xv.rearrange("p (g u n e) -> p n g u e", g=G, u=2, e=2),
+                in1=xs[:].rearrange("p (g u e) -> p g u e", u=2, e=2).unsqueeze(1).to_broadcast([P, P, G, 2, 2]),
+                op=ALU.mult,
+            )
+            st["xg", n] = xg
+
+        def quant_x(n):
+            xg = st.pop(("xg", n))
+            xq = work.tile([P, G * P], U32, name="xq", align_bytes=64)
+            xqs = work.tile([P, G * P], U8, name="xqs", align_bytes=64)
+            nc.vector.quantize_mx(out=xq[:].bitcast(FP8X4), scales=xqs[:], in_=xg[:])
+            st["xq", n] = (xq, xqs)
+
+        def mm_down(n):
+            xq, xqs = st.pop(("xq", n))
+            lat = psum.tile([P, PACK * P], F32, name="lat")
+            for t in range(PACK):
+                for g in range(G):
+                    c = slice(t * P, (t + 1) * P)
+                    nc.tensor.matmul_mx(
+                        out=lat[:, c],
+                        lhsT=wd[:, g * R + t * P : g * R + (t + 1) * P].bitcast(FP8X4),
+                        lhsT_scale=wds[:, g, c],
+                        rhs=xq[:, g * P : (g + 1) * P].bitcast(FP8X4),
+                        rhs_scale=xqs[:, g * P : (g + 1) * P],
+                        start=(g == 0),
+                        stop=(g == G - 1),
+                    )
+            st["lat", n] = lat
+
+        def lat_out(n):
+            lat = st.pop(("lat", n))
+            lg = work.tile([P, PACK * P], BF16, name="lg", align_bytes=64)
+            nc.scalar.copy(
+                out=lg[:].rearrange("p (n t) -> p n t", t=PACK), in_=lat[:].rearrange("p (t n) -> p n t", t=PACK)
+            )
+            st["lg", n] = lg
+
+        def quant_l(n):
+            lg = st.pop(("lg", n))
+            lq = work.tile([P, P], U32, name="lq", align_bytes=64)
+            lqs = work.tile([P, P], U8, name="lqs", align_bytes=64)
+            nc.vector.quantize_mx(out=lq[:].bitcast(FP8X4), scales=lqs[:], in_=lg[:])
+            st["lq", n] = (lq, lqs)
+
+        def mm_up(n):
+            lq, lqs = st.pop(("lq", n))
+            kp = psum.tile([P, HD], F32, name="kp")
+            vp = psum.tile([P, HD], F32, name="vp")
+            for half, dst in enumerate((kp, vp)):
+                c = slice(half * HD, (half + 1) * HD)
+                nc.tensor.matmul_mx(
+                    out=dst[:],
+                    lhsT=lq[:].bitcast(FP8X4),
+                    lhsT_scale=lqs[:],
+                    rhs=wu[:, c].bitcast(FP8X4),
+                    rhs_scale=wus[:, c],
+                    start=True,
+                    stop=True,
+                )
+            st["kp", n] = kp
+            st["vp", n] = vp
+
+        def squares(n):
+            kp = st["kp", n]
+            ss = work.tile([P, H], F32, name="ss")
+            rms = work.tile([P, H], F32, name="rms")
+            junk = work.tile([P, D], BF16, name="junk")
+            for h in range(H):
+                nc.scalar.activation(
+                    out=junk[:], in_=kp[:, h * D : (h + 1) * D], func=ACT.Square, accum_out=ss[:, h : h + 1]
+                )
+            nc.scalar.activation(out=rms[:], in_=ss[:], func=ACT.Sqrt, scale=1.0 / D, bias=EPS)
+            st["rms", n] = rms
+
+        def v_out(n):
+            vp = st.pop(("vp", n))
+            if n % 2 == 0:
+                st["vs"] = store.tile([P, 2, HD], F32, name="vs")
+            vs = st["vs"]
+            nc.scalar.copy(out=vs[:, n % 2, :], in_=vp[:])
+            put(out_v, vs, n)
+
+        def put(out, tile, n):
+            if n % 2 == 1:
+                b, i = divmod(n - 1, IT)
+                nc.sync.dma_start(
+                    out=out[b].rearrange("(p i) h d -> p i (h d)", i=IT)[:, i : i + 2, :], in_=tile[:]
+                )
+
+        def products(n):
+            kp = st.pop(("kp", n))
+            rms = st.pop(("rms", n))
+            rstd = work.tile([P, H], F32, name="rstd")
+            nc.vector.reciprocal(out=rstd[:], in_=rms[:])
+            t1 = work.tile([P, HD], F32, name="t1")
+            t2 = work.tile([P, HD], F32, name="t2")
+            st["t", n] = (t1, t2)
+            if n < NT - 1:
+                heads(n, kp, rstd, t1, t2, range(H))
+                add(n, nc.gpsimd, slice(0, HD))
+            else:
+                heads(n, kp, rstd, t1, t2, range(H // 2))
+                add(n, nc.gpsimd, slice(0, HD // 2))
+                heads(n, kp, rstd, t1, t2, range(H // 2, H))
+                add(n, nc.vector, slice(HD // 2, HD))
+
+        def heads(n, kp, rstd, t1, t2, hs):
+            i = n % IT
+            for h in hs:
+                c = slice(h * D, (h + 1) * D)
+                nc.vector.scalar_tensor_tensor(
+                    out=t1[:, c], in0=kp[:, c], scalar=rstd[:, h : h + 1], in1=ta[:, i, :], op0=ALU.mult, op1=ALU.mult
+                )
+                nc.vector.scalar_tensor_tensor(
+                    out=t2[:, c].rearrange("p (j e) -> p j e", e=2),
+                    in0=kp[:, c].rearrange("p (j e) -> p j e", e=2)[:, :, ::-1],
+                    scalar=rstd[:, h : h + 1],
+                    in1=tb[:, i, :].rearrange("p (j e) -> p j e", e=2),
+                    op0=ALU.mult,
+                    op1=ALU.mult,
+                )
+
+        def add(n, eng, c):
+            t1, t2 = st["t", n]
+            if n % 2 == 0:
+                st["ks"] = store.tile([P, 2, HD], F32, name="ks")
+            ks = st["ks"]
+            eng.tensor_tensor(out=ks[:, n % 2, c], in0=t1[:, c], in1=t2[:, c], op=ALU.add)
+            if n < NT - 2:
+                put(out_k, ks, n)
+            else:
+                b, i = divmod(n, IT)
+                nc.sync.dma_start(
+                    out=out_k[b].rearrange("(p i) h d -> p i (h d)", i=IT)[:, i, c], in_=ks[:, n % 2, c]
+                )
+
+        def do(stage, n):
+            if 0 <= n < NT:
+                stage(n)
+
+        for s in range(-5, NT):
+            do(cast, s + 5)
+            do(turn, s + 4)
+            do(quant_x, s + 2)
+            do(mm_down, s + 2)
+            do(quant_l, s + 1)
+            do(mm_up, s + 1)
+            do(scale, s + 3)
+            do(lat_out, s + 2)
+            do(squares, s + 1)
+            do(v_out, s + 1)
+            do(products, s)

@@ -20,7 +20,7 @@ ALU = mybir.AluOpType
 P = 128
 PACK = 4
 IT = T // P
-NT = B * IT
+NP = B * IT // 2
 HD = H * D
 G = C // (P * PACK)
 
@@ -33,14 +33,14 @@ def tile_mla_pa_t_w8_kernel(
         keep = ctx.enter_context(tc.tile_pool(name="keep", bufs=1))
         work = ctx.enter_context(tc.tile_pool(name="work", bufs=3))
         store = ctx.enter_context(tc.tile_pool(name="store", bufs=3))
-        psum = ctx.enter_context(tc.psum_pool(name="psum", bufs=2))
+        psum = ctx.enter_context(tc.psum_pool(name="psum", bufs=1))
         ctx.enter_context(tc.manual_schedule())
 
         warm = keep.tile([P, 1], F32, name="warm")
         nc.vector.memset(warm[:], 1.0)
         nc.scalar.activation(out=warm[:], in_=warm[:], func=ACT.Sqrt)
 
-        loads = [(0, 0, 1), (0, 1, 1), (0, 2, 2), (0, 4, 4)]
+        loads = [(0, 0, 2), (0, 2, 2), (0, 4, 4)]
         loads += [(b, i, 4) for b in range(1, B) for i in (0, 4)]
         bytes_of = {}
 
@@ -48,8 +48,8 @@ def tile_mla_pa_t_w8_kernel(
             b, i0, n = entry
             xb = keep.tile([P, n, C], U8, name="xbytes_%d_%d" % (b, i0))
             nc.sync.dma_start(out=xb[:], in_=x_bytes[b].rearrange("(p i) k -> p i k", i=IT)[:, i0 : i0 + n, :])
-            for i in range(n):
-                bytes_of[b * IT + i0 + i] = (xb, i)
+            for i in range(0, n, 2):
+                bytes_of[(b * IT + i0 + i) // 2] = (xb, i)
 
         load_x(loads[0])
         wds_raw = keep.tile([P, G, R], U8, name="wds_raw", align_bytes=64)
@@ -71,10 +71,9 @@ def tile_mla_pa_t_w8_kernel(
             nc.sync.dma_start(
                 out=wus[32 * q : 32 * q + 4, :].bitcast(I32), in_=wu_scales[0, 4 * q : 4 * q + 4, :].bitcast(I32)
             )
-        load_x(loads[2])
         wu = keep.tile([P, 2 * HD], I32, name="wu", align_bytes=64)
         nc.sync.dma_start(out=wu[:], in_=wu_words[0].rearrange("p n t -> p (n t)").bitcast(I32))
-        for entry in loads[3:]:
+        for entry in loads[2:]:
             load_x(entry)
 
         xs = keep.tile([P, G * PACK], F32, name="xs")
@@ -92,17 +91,34 @@ def tile_mla_pa_t_w8_kernel(
         ident = keep.tile([P, P], F32, name="ident")
         make_identity(nc, ident[:])
 
-        wd = keep.tile([P, G * R], I32, name="wd", align_bytes=64)
         st = {}
+
+        def cast(n, a, lo, hi, eng):
+            xb, i = bytes_of[n]
+            if ("xw", n, a) not in st:
+                st["xw", n, a] = work.tile([P, C], BF16, name="xw%d" % a)
+            xw = st["xw", n, a]
+            if eng == "v":
+                nc.vector.tensor_copy(out=xw[:, lo:hi], in_=xb[:, i + a, lo:hi].bitcast(FP8))
+            else:
+                nc.scalar.copy(out=xw[:, lo:hi], in_=xb[:, i + a, lo:hi].bitcast(FP8))
+
+        for g in range(G):
+            cast(0, 0, g * 512, (g + 1) * 512, "v")
+            cast(0, 1, g * 512, (g + 1) * 512, "s")
+
+        wd = keep.tile([P, G * R], I32, name="wd", align_bytes=64)
         wds = keep.tile([P, G, R], U8, name="wds", align_bytes=64)
         for t in range(PACK):
             eng = nc.gpsimd if t < 2 else nc.vector
             eng.tensor_copy(out=wds[:, :, t * P : (t + 1) * P], in_=wds_raw[:, :, t::PACK])
-        for g in range(G):
-            nc.vector.tensor_copy(
-                out=wd[:, g * R : (g + 1) * R].rearrange("p (t m) -> p t m", t=PACK),
-                in_=wd_raw[:, g * R : (g + 1) * R].rearrange("p (m t) -> p t m", t=PACK),
-            )
+
+        def permute_wd():
+            for g in range(G):
+                nc.vector.tensor_copy(
+                    out=wd[:, g * R : (g + 1) * R].rearrange("p (t m) -> p t m", t=PACK),
+                    in_=wd_raw[:, g * R : (g + 1) * R].rearrange("p (m t) -> p t m", t=PACK),
+                )
 
         gain_x = keep.tile([P, D], F32, name="gain_x")
         ta = keep.tile([P, IT, D], F32, name="ta")
@@ -119,181 +135,222 @@ def tile_mla_pa_t_w8_kernel(
                 op=ALU.mult,
             )
 
+        def turn(n, g):
+            xt = psum.tile([P, 2, 2, P], F32, name="xt%d" % g)
+            for u in range(2):
+                for a in range(2):
+                    words = st["xw", n, a][:].bitcast(F32)
+                    nc.tensor.transpose(xt[:, u, a, :], words[:, 256 * g + u : 256 * (g + 1) : 2], ident[:])
+            st["xt", n, g] = xt
 
-        def cast(n):
-            xb, i = bytes_of[n]
-            xw = work.tile([P, C], BF16, name="xw")
-            if n == 0:
-                nc.vector.tensor_copy(out=xw[:, : C // 2], in_=xb[:, i, : C // 2].bitcast(FP8))
-                nc.scalar.copy(out=xw[:, C // 2 :], in_=xb[:, i, C // 2 :].bitcast(FP8))
-            else:
-                nc.scalar.copy(out=xw[:], in_=xb[:, i, :].bitcast(FP8))
-            st["xw", n] = xw
-
-        def turn(n):
-            words = st.pop(("xw", n))[:].bitcast(F32)
-            xt = psum.tile([P, 2 * G, P], F32, name="xt")
-            for g in range(G):
-                for u in range(2):
-                    nc.tensor.transpose(xt[:, 2 * g + u, :], words[:, 256 * g + u : 256 * (g + 1) : 2], ident[:])
-            st["xt", n] = xt
-
-        def scale(n):
-            xt = st.pop(("xt", n))
-            xv = xt[:].rearrange("p a n -> p (a n)").bitcast(BF16)
-            xg = work.tile([P, G * 512], BF16, name="xg", align_bytes=64)
+        def scale(n, g):
+            xt = st.pop(("xt", n, g))
+            if g == 0:
+                st["xg", n] = work.tile([P, G * 1024], BF16, name="xg", align_bytes=64)
+            xg = st["xg", n]
             nc.vector.tensor_tensor(
-                out=xg[:].rearrange("p (g n u e) -> p n g u e", g=G, u=2, e=2),
-                in0=xv.rearrange("p (g u n e) -> p n g u e", g=G, u=2, e=2),
-                in1=xs[:].rearrange("p (g u e) -> p g u e", u=2, e=2).unsqueeze(1).to_broadcast([P, P, G, 2, 2]),
+                out=xg[:, g * 1024 : (g + 1) * 1024].rearrange("p (n u e) -> p n u e", u=2, e=2),
+                in0=xs[:, g * PACK : (g + 1) * PACK]
+                .rearrange("p (u e) -> p u e", e=2)
+                .unsqueeze(1)
+                .to_broadcast([P, 2 * P, 2, 2]),
+                in1=xt[:].rearrange("p u a n -> p (u a n)").bitcast(BF16).rearrange("p (u n e) -> p n u e", u=2, e=2),
                 op=ALU.mult,
             )
-            st["xg", n] = xg
 
         def quant_x(n):
             xg = st.pop(("xg", n))
-            xq = work.tile([P, G * P], U32, name="xq", align_bytes=64)
-            xqs = work.tile([P, G * P], U8, name="xqs", align_bytes=64)
+            xq = work.tile([P, G * 2 * P], U32, name="xq", align_bytes=64)
+            xqs = work.tile([P, G * 2 * P], U8, name="xqs", align_bytes=64)
             nc.vector.quantize_mx(out=xq[:].bitcast(FP8X4), scales=xqs[:], in_=xg[:])
             st["xq", n] = (xq, xqs)
 
-        def mm_down(n):
-            xq, xqs = st.pop(("xq", n))
-            lat = psum.tile([P, PACK * P], F32, name="lat")
+        def mm_down(n, a):
+            xq, xqs = st["xq", n]
+            lat = psum.tile([P, PACK * P], F32, name="lat%d" % a)
             for t in range(PACK):
                 for g in range(G):
                     c = slice(t * P, (t + 1) * P)
+                    m = slice((2 * g + a) * P, (2 * g + a + 1) * P)
                     nc.tensor.matmul_mx(
                         out=lat[:, c],
                         lhsT=wd[:, g * R + t * P : g * R + (t + 1) * P].bitcast(FP8X4),
                         lhsT_scale=wds[:, g, c],
-                        rhs=xq[:, g * P : (g + 1) * P].bitcast(FP8X4),
-                        rhs_scale=xqs[:, g * P : (g + 1) * P],
+                        rhs=xq[:, m].bitcast(FP8X4),
+                        rhs_scale=xqs[:, m],
                         start=(g == 0),
                         stop=(g == G - 1),
                     )
-            st["lat", n] = lat
+            st["lat", n, a] = lat
 
-        def lat_out(n):
-            lat = st.pop(("lat", n))
-            lg = work.tile([P, PACK * P], BF16, name="lg", align_bytes=64)
+        def lat_out(n, a):
+            lat = st.pop(("lat", n, a))
+            if a == 0:
+                st["lg", n] = work.tile([P, 2 * PACK * P], BF16, name="lg", align_bytes=64)
+            lg = st["lg", n]
             nc.scalar.copy(
-                out=lg[:].rearrange("p (n t) -> p n t", t=PACK), in_=lat[:].rearrange("p (t n) -> p n t", t=PACK)
+                out=lg[:, a * 512 : (a + 1) * 512].rearrange("p (n t) -> p n t", t=PACK),
+                in_=lat[:].rearrange("p (t n) -> p n t", t=PACK),
             )
-            st["lg", n] = lg
 
         def quant_l(n):
             lg = st.pop(("lg", n))
-            lq = work.tile([P, P], U32, name="lq", align_bytes=64)
-            lqs = work.tile([P, P], U8, name="lqs", align_bytes=64)
+            lq = work.tile([P, 2 * P], U32, name="lq", align_bytes=64)
+            lqs = work.tile([P, 2 * P], U8, name="lqs", align_bytes=64)
             nc.vector.quantize_mx(out=lq[:].bitcast(FP8X4), scales=lqs[:], in_=lg[:])
             st["lq", n] = (lq, lqs)
 
-        def mm_up(n):
-            lq, lqs = st.pop(("lq", n))
-            kp = psum.tile([P, HD], F32, name="kp")
-            vp = psum.tile([P, HD], F32, name="vp")
-            for half, dst in enumerate((kp, vp)):
-                c = slice(half * HD, (half + 1) * HD)
-                nc.tensor.matmul_mx(
-                    out=dst[:],
-                    lhsT=lq[:].bitcast(FP8X4),
-                    lhsT_scale=lqs[:],
-                    rhs=wu[:, c].bitcast(FP8X4),
-                    rhs_scale=wus[:, c],
-                    start=True,
-                    stop=True,
-                )
-            st["kp", n] = kp
-            st["vp", n] = vp
+        def mm_up(n, a, half):
+            lq, lqs = st["lq", n]
+            dst = psum.tile([P, HD], F32, name="%s%d" % ("kv"[half], a))
+            c = slice(half * HD, (half + 1) * HD)
+            m = slice(a * P, (a + 1) * P)
+            nc.tensor.matmul_mx(
+                out=dst[:],
+                lhsT=lq[:, m].bitcast(FP8X4),
+                lhsT_scale=lqs[:, m],
+                rhs=wu[:, c].bitcast(FP8X4),
+                rhs_scale=wus[:, c],
+                start=True,
+                stop=True,
+            )
+            st["kv"[half], n, a] = dst
 
-        def squares(n):
-            kp = st["kp", n]
-            ss = work.tile([P, H], F32, name="ss")
-            rms = work.tile([P, H], F32, name="rms")
+        def dummy(n):
+            junk = psum.tile([P, HD], F32, name="lat1")
+            nc.tensor.matmul_mx(
+                out=junk[:],
+                lhsT=wd[:, :P].bitcast(FP8X4),
+                lhsT_scale=wds[:, 0, :P],
+                rhs=wu[:, :HD].bitcast(FP8X4),
+                rhs_scale=wus[:, :HD],
+                start=True,
+                stop=True,
+            )
+
+        def squares(n, a):
+            kp = st["k", n, a]
+            ss = work.tile([P, H], F32, name="ss%d" % a)
             junk = work.tile([P, D], BF16, name="junk")
             for h in range(H):
                 nc.scalar.activation(
                     out=junk[:], in_=kp[:, h * D : (h + 1) * D], func=ACT.Square, accum_out=ss[:, h : h + 1]
                 )
-            nc.scalar.activation(out=rms[:], in_=ss[:], func=ACT.Sqrt, scale=1.0 / D, bias=EPS)
-            st["rms", n] = rms
+            st["ss", n, a] = ss
 
-        def v_out(n):
-            vp = st.pop(("vp", n))
-            if n % 2 == 0:
+        def rsqrt(n, a):
+            ss = st.pop(("ss", n, a))
+            rstd = work.tile([P, H], F32, name="rstd%d" % a)
+            nc.scalar.activation(out=rstd[:], in_=ss[:], func=ACT.Abs_reciprocal_sqrt, scale=1.0 / D, bias=EPS)
+            st["rstd", n, a] = rstd
+
+        def v_out(n, a):
+            vp = st.pop(("v", n, a))
+            if a == 0:
                 st["vs"] = store.tile([P, 2, HD], F32, name="vs")
             vs = st["vs"]
-            nc.scalar.copy(out=vs[:, n % 2, :], in_=vp[:])
-            put(out_v, vs, n)
+            nc.scalar.copy(out=vs[:, a, :], in_=vp[:])
+            if a == 1:
+                put(out_v, vs, n)
 
         def put(out, tile, n):
-            if n % 2 == 1:
-                b, i = divmod(n - 1, IT)
-                nc.sync.dma_start(
-                    out=out[b].rearrange("(p i) h d -> p i (h d)", i=IT)[:, i : i + 2, :], in_=tile[:]
-                )
+            b, i = divmod(2 * n, IT)
+            nc.sync.dma_start(out=out[b].rearrange("(p i) h d -> p i (h d)", i=IT)[:, i : i + 2, :], in_=tile[:])
 
-        def products(n):
-            kp = st.pop(("kp", n))
-            rms = st.pop(("rms", n))
-            rstd = work.tile([P, H], F32, name="rstd")
-            nc.vector.reciprocal(out=rstd[:], in_=rms[:])
-            t1 = work.tile([P, HD], F32, name="t1")
-            t2 = work.tile([P, HD], F32, name="t2")
-            st["t", n] = (t1, t2)
-            if n < NT - 1:
-                heads(n, kp, rstd, t1, t2, range(H))
-                add(n, nc.gpsimd, slice(0, HD))
-            else:
-                heads(n, kp, rstd, t1, t2, range(H // 2))
-                add(n, nc.gpsimd, slice(0, HD // 2))
-                heads(n, kp, rstd, t1, t2, range(H // 2, H))
-                add(n, nc.vector, slice(HD // 2, HD))
-
-        def heads(n, kp, rstd, t1, t2, hs):
-            i = n % IT
+        def products(n, a, hs):
+            kp = st["k", n, a]
+            rstd = st["rstd", n, a]
+            if ("t", n, a) not in st:
+                t1 = work.tile([P, HD], F32, name="t1")
+                t2 = work.tile([P, HD], F32, name="t2")
+                st["t", n, a] = (t1, t2)
+            t1, t2 = st["t", n, a]
+            i = (2 * n + a) % IT
             for h in hs:
                 c = slice(h * D, (h + 1) * D)
                 nc.vector.scalar_tensor_tensor(
-                    out=t1[:, c], in0=kp[:, c], scalar=rstd[:, h : h + 1], in1=ta[:, i, :], op0=ALU.mult, op1=ALU.mult
+                    out=t1[:, c], in0=ta[:, i, :], scalar=rstd[:, h : h + 1], in1=kp[:, c], op0=ALU.mult, op1=ALU.mult
                 )
                 nc.vector.scalar_tensor_tensor(
                     out=t2[:, c].rearrange("p (j e) -> p j e", e=2),
-                    in0=kp[:, c].rearrange("p (j e) -> p j e", e=2)[:, :, ::-1],
+                    in0=tb[:, i, :].rearrange("p (j e) -> p j e", e=2),
                     scalar=rstd[:, h : h + 1],
-                    in1=tb[:, i, :].rearrange("p (j e) -> p j e", e=2),
+                    in1=kp[:, c].rearrange("p (j e) -> p j e", e=2)[:, :, ::-1],
                     op0=ALU.mult,
                     op1=ALU.mult,
                 )
 
-        def add(n, eng, c):
-            t1, t2 = st["t", n]
-            if n % 2 == 0:
-                st["ks"] = store.tile([P, 2, HD], F32, name="ks")
-            ks = st["ks"]
-            eng.tensor_tensor(out=ks[:, n % 2, c], in0=t1[:, c], in1=t2[:, c], op=ALU.add)
-            if n < NT - 2:
-                put(out_k, ks, n)
+        def add(n, a, eng, c):
+            t1, t2 = st["t", n, a]
+            if ("ks", n) not in st:
+                st["ks", n] = store.tile([P, 2, HD], F32, name="ks")
+            ks = st["ks", n]
+            eng.tensor_tensor(out=ks[:, a, c], in0=t1[:, c], in1=t2[:, c], op=ALU.add)
+            if n < NP - 1:
+                if a == 1:
+                    put(out_k, ks, n)
             else:
-                b, i = divmod(n, IT)
-                nc.sync.dma_start(
-                    out=out_k[b].rearrange("(p i) h d -> p i (h d)", i=IT)[:, i, c], in_=ks[:, n % 2, c]
-                )
+                b, i = divmod(2 * n + a, IT)
+                nc.sync.dma_start(out=out_k[b].rearrange("(p i) h d -> p i (h d)", i=IT)[:, i, c], in_=ks[:, a, c])
 
-        def do(stage, n):
-            if 0 <= n < NT:
-                stage(n)
+        full = slice(0, HD)
+        lo, hi = slice(0, HD // 2), slice(HD // 2, HD)
 
-        for s in range(-5, NT):
-            do(cast, s + 5)
-            do(turn, s + 4)
-            do(quant_x, s + 2)
-            do(mm_down, s + 2)
-            do(quant_l, s + 1)
-            do(mm_up, s + 1)
-            do(scale, s + 3)
-            do(lat_out, s + 2)
-            do(squares, s + 1)
-            do(v_out, s + 1)
-            do(products, s)
+        def ok(n):
+            return 0 <= n < NP
+
+        for p in range(-5, NP):
+            if ok(p + 1):
+                quant_l(p + 1)
+                for a in range(2):
+                    mm_up(p + 1, a, 1)
+                v_out(p + 1, 0)
+            if ok(p):
+                rsqrt(p, 1)
+            if ok(p + 1):
+                v_out(p + 1, 1)
+            if ok(p + 2):
+                quant_x(p + 2)
+                if p + 2 == 0:
+                    permute_wd()
+                for a in range(2):
+                    mm_down(p + 2, a)
+                for a in range(2):
+                    lat_out(p + 2, a)
+            if ok(p):
+                products(p, 0, range(H))
+                add(p, 0, nc.gpsimd, full)
+            if ok(p + 1):
+                mm_up(p + 1, 0, 0)
+                squares(p + 1, 0)
+            if 0 < p + 5 < NP:
+                cast(p + 5, 0, 0, C, "s")
+            if ok(p + 1):
+                rsqrt(p + 1, 0)
+            if 0 < p + 5 < NP:
+                cast(p + 5, 1, 0, C, "s")
+            if ok(p + 3):
+                scale(p + 3, 0)
+            if ok(p) and ok(p + 1):
+                dummy(p)
+            if ok(p + 4):
+                turn(p + 4, 0)
+            if ok(p) and ok(p + 1):
+                dummy(p)
+            if ok(p) and p < NP - 1:
+                products(p, 1, range(H))
+                add(p, 1, nc.gpsimd, full)
+            elif ok(p):
+                products(p, 1, range(H // 2))
+                add(p, 1, nc.gpsimd, lo)
+                products(p, 1, range(H // 2, H))
+                add(p, 1, nc.vector, hi)
+            if ok(p + 1):
+                mm_up(p + 1, 1, 0)
+                squares(p + 1, 1)
+            if ok(p) and ok(p + 1):
+                dummy(p)
+            if ok(p + 3):
+                scale(p + 3, 1)
+            if ok(p + 4):
+                turn(p + 4, 1)

@@ -231,10 +231,10 @@ def tile_mla_pa_t_w8_kernel(
         def squares(n, a):
             kp = st["k", n, a]
             ss = work.tile([P, H], F32, name="ss%d" % a)
-            junk = work.tile([P, D], BF16, name="junk")
+            junk = work.tile([P, HD], BF16, name="junk")
             for h in range(H):
                 nc.scalar.activation(
-                    out=junk[:], in_=kp[:, h * D : (h + 1) * D], func=ACT.Square, accum_out=ss[:, h : h + 1]
+                    out=junk[:, h * D : (h + 1) * D], in_=kp[:, h * D : (h + 1) * D], func=ACT.Square, accum_out=ss[:, h : h + 1]
                 )
             st["ss", n, a] = ss
 

@@ -31,8 +31,8 @@ def tile_mla_pa_t_w8_kernel(
     nc = tc.nc
     with ExitStack() as ctx:
         keep = ctx.enter_context(tc.tile_pool(name="keep", bufs=1))
-        work = ctx.enter_context(tc.tile_pool(name="work", bufs=3))
-        store = ctx.enter_context(tc.tile_pool(name="store", bufs=3))
+        work = ctx.enter_context(tc.tile_pool(name="work", bufs=4))
+        store = ctx.enter_context(tc.tile_pool(name="store", bufs=4))
         psum = ctx.enter_context(tc.psum_pool(name="psum", bufs=1))
         ctx.enter_context(tc.manual_schedule())
 
@@ -108,10 +108,10 @@ def tile_mla_pa_t_w8_kernel(
             cast(0, 1, g * 512, (g + 1) * 512, "s")
 
         wd = keep.tile([P, G * R], I32, name="wd", align_bytes=64)
-        wds = keep.tile([P, G, R], U8, name="wds", align_bytes=64)
+        wds = keep.tile([P, PACK, G, P], U8, name="wds", align_bytes=64)
         for t in range(PACK):
             eng = nc.gpsimd if t < 2 else nc.vector
-            eng.tensor_copy(out=wds[:, :, t * P : (t + 1) * P], in_=wds_raw[:, :, t::PACK])
+            eng.tensor_copy(out=wds[:, t, :, :], in_=wds_raw[:, :, t::PACK])
 
         def permute_wd():
             for g in range(G):
@@ -175,7 +175,7 @@ def tile_mla_pa_t_w8_kernel(
                     nc.tensor.matmul_mx(
                         out=lat[:, c],
                         lhsT=wd[:, g * R + t * P : g * R + (t + 1) * P].bitcast(FP8X4),
-                        lhsT_scale=wds[:, g, c],
+                        lhsT_scale=wds[:, t, g, :],
                         rhs=xq[:, m].bitcast(FP8X4),
                         rhs_scale=xqs[:, m],
                         start=(g == 0),
@@ -221,7 +221,7 @@ def tile_mla_pa_t_w8_kernel(
             nc.tensor.matmul_mx(
                 out=junk[:],
                 lhsT=wd[:, :P].bitcast(FP8X4),
-                lhsT_scale=wds[:, 0, :P],
+                lhsT_scale=wds[:, 0, 0, :],
                 rhs=wu[:, :HD].bitcast(FP8X4),
                 rhs_scale=wus[:, :HD],
                 start=True,
@@ -257,6 +257,8 @@ def tile_mla_pa_t_w8_kernel(
             b, i = divmod(2 * n, IT)
             nc.sync.dma_start(out=out[b].rearrange("(p i) h d -> p i (h d)", i=IT)[:, i : i + 2, :], in_=tile[:])
 
+        H_STT, H_ACT, H_POOL = 0, 0, 4
+
         def products(n, a, hs):
             kp = st["k", n, a]
             rstd = st["rstd", n, a]
@@ -266,7 +268,25 @@ def tile_mla_pa_t_w8_kernel(
                 st["t", n, a] = (t1, t2)
             t1, t2 = st["t", n, a]
             i = (2 * n + a) % IT
+            plain = [h for h in hs if h >= H_STT]
+            if plain:
+                m = len(plain)
+                c = slice(plain[0] * D, (plain[-1] + 1) * D)
+                nc.vector.tensor_tensor(
+                    out=t1[:, c].rearrange("p (h d) -> p h d", d=D),
+                    in0=ta[:, i : i + 1, :].to_broadcast([P, m, D]),
+                    in1=kp[:, c].rearrange("p (h d) -> p h d", d=D),
+                    op=ALU.mult,
+                )
+                nc.vector.tensor_tensor(
+                    out=t2[:, c].rearrange("p (h j e) -> p h j e", j=D // 2, e=2),
+                    in0=tb[:, i : i + 1, :].rearrange("p h (j e) -> p h j e", e=2).to_broadcast([P, m, D // 2, 2]),
+                    in1=kp[:, c].rearrange("p (h j e) -> p h j e", j=D // 2, e=2)[:, :, :, ::-1],
+                    op=ALU.mult,
+                )
             for h in hs:
+                if h >= H_STT:
+                    continue
                 c = slice(h * D, (h + 1) * D)
                 nc.vector.scalar_tensor_tensor(
                     out=t1[:, c], in0=ta[:, i, :], scalar=rstd[:, h : h + 1], in1=kp[:, c], op0=ALU.mult, op1=ALU.mult
@@ -285,19 +305,47 @@ def tile_mla_pa_t_w8_kernel(
             if ("ks", n) not in st:
                 st["ks", n] = store.tile([P, 2, HD], F32, name="ks")
             ks = st["ks", n]
-            eng.tensor_tensor(out=ks[:, a, c], in0=t1[:, c], in1=t2[:, c], op=ALU.add)
-            if n < NP - 1:
-                if a == 1:
-                    put(out_k, ks, n)
-            else:
-                b, i = divmod(2 * n + a, IT)
-                nc.sync.dma_start(out=out_k[b].rearrange("(p i) h d -> p i (h d)", i=IT)[:, i, c], in_=ks[:, a, c])
+            w = (c.stop - c.start) // 1
+            for c0 in range(c.start, c.stop, w):
+                eng.tensor_tensor(
+                    out=ks[:, a, c0 : c0 + w], in0=t1[:, c0 : c0 + w], in1=t2[:, c0 : c0 + w], op=ALU.add
+                )
+
+        def final(n, a, hs, who):
+            ks = st["ks", n]
+            rstd = st["rstd", n, a]
+            for h in hs:
+                c = slice(h * D, (h + 1) * D)
+                if who == "s":
+                    nc.scalar.activation(out=ks[:, a, c], in_=ks[:, a, c], func=ACT.Copy, scale=rstd[:, h : h + 1])
+                elif who == "v":
+                    nc.vector.tensor_scalar(
+                        out=ks[:, a, c], in0=ks[:, a, c], scalar1=rstd[:, h : h + 1], scalar2=None, op0=ALU.mult
+                    )
+                else:
+                    nc.gpsimd.tensor_scalar(
+                        out=ks[:, a, c], in0=ks[:, a, c], scalar1=rstd[:, h : h + 1], scalar2=0.0, op0=ALU.mult, op1=ALU.add
+                    )
+
+        def put_k(n, a, c):
+            ks = st["ks", n]
+            b, i = divmod(2 * n + a, IT)
+            nc.sync.dma_start(out=out_k[b].rearrange("(p i) h d -> p i (h d)", i=IT)[:, i, c], in_=ks[:, a, c])
 
         full = slice(0, HD)
         lo, hi = slice(0, HD // 2), slice(HD // 2, HD)
 
         def ok(n):
             return 0 <= n < NP
+
+        TAIL = 2
+
+        def fin_heads(n, who):
+            act = H if n >= NP - TAIL else H_ACT
+            return range(act) if who == "s" else range(act, H)
+
+        def adder(n, a):
+            return nc.vector if n >= NP - TAIL and a == 1 else nc.gpsimd
 
         for p in range(-5, NP):
             if ok(p + 1):
@@ -307,6 +355,8 @@ def tile_mla_pa_t_w8_kernel(
                 v_out(p + 1, 0)
             if ok(p):
                 rsqrt(p, 1)
+            if ok(p - 1):
+                final(p - 1, 1, fin_heads(p - 1, "s"), "s")
             if ok(p + 1):
                 v_out(p + 1, 1)
             if ok(p + 2):
@@ -319,7 +369,10 @@ def tile_mla_pa_t_w8_kernel(
                     lat_out(p + 2, a)
             if ok(p):
                 products(p, 0, range(H))
-                add(p, 0, nc.gpsimd, full)
+                add(p, 0, adder(p, 0), full)
+            if ok(p - 1):
+                final(p - 1, 1, fin_heads(p - 1, "g"), "g")
+                put(out_k, st["ks", p - 1], p - 1)
             if ok(p + 1):
                 mm_up(p + 1, 0, 0)
                 squares(p + 1, 0)
@@ -339,15 +392,24 @@ def tile_mla_pa_t_w8_kernel(
                 dummy(p)
             if ok(p) and p < NP - 1:
                 products(p, 1, range(H))
-                add(p, 1, nc.gpsimd, full)
+                add(p, 1, adder(p, 1), full)
+                final(p, 0, fin_heads(p, "g"), "g")
             elif ok(p):
                 products(p, 1, range(H // 2))
                 add(p, 1, nc.gpsimd, lo)
+                final(p, 0, range(H), "s")
+                put_k(p, 0, full)
                 products(p, 1, range(H // 2, H))
                 add(p, 1, nc.vector, hi)
+                final(p, 1, range(H // 2), "s")
+                put_k(p, 1, lo)
+                final(p, 1, range(H // 2, H), "s")
+                put_k(p, 1, hi)
             if ok(p + 1):
                 mm_up(p + 1, 1, 0)
                 squares(p + 1, 1)
+            if ok(p) and p < NP - 1:
+                final(p, 0, fin_heads(p, "s"), "s")
             if ok(p) and ok(p + 1):
                 dummy(p)
             if ok(p + 3):

@@ -61,19 +61,20 @@ def tile_mla_pa_t_w8_kernel(
                 out=wds_raw[32 * q : 32 * q + 4, :, :].bitcast(I32),
                 in_=wd_scales[:, 4 * q : 4 * q + 4, :].rearrange("g q n -> q g n").bitcast(I32),
             )
+        load_x(loads[1])
         wd_raw = keep.tile([P, G * R], I32, name="wd_raw", align_bytes=64)
         for g in range(G):
             nc.sync.dma_start(
                 out=wd_raw[:, g * R : (g + 1) * R], in_=wd_words[g].rearrange("p n t -> p (n t)").bitcast(I32)
             )
-        load_x(loads[1])
+        load_x(loads[2])
         for q in range(4):
             nc.sync.dma_start(
                 out=wus[32 * q : 32 * q + 4, :].bitcast(I32), in_=wu_scales[0, 4 * q : 4 * q + 4, :].bitcast(I32)
             )
         wu = keep.tile([P, 2 * HD], I32, name="wu", align_bytes=64)
         nc.sync.dma_start(out=wu[:], in_=wu_words[0].rearrange("p n t -> p (n t)").bitcast(I32))
-        for entry in loads[2:]:
+        for entry in loads[3:]:
             load_x(entry)
 
         xs = keep.tile([P, G * PACK], F32, name="xs")
@@ -109,11 +110,12 @@ def tile_mla_pa_t_w8_kernel(
 
         wd = keep.tile([P, G * R], I32, name="wd", align_bytes=64)
         wds = keep.tile([P, PACK, G, P], U8, name="wds", align_bytes=64)
-        for t in range(PACK):
-            eng = nc.gpsimd if t < 2 else nc.vector
-            eng.tensor_copy(out=wds[:, t, :, :], in_=wds_raw[:, :, t::PACK])
+        for t in range(2):
+            nc.vector.tensor_copy(out=wds[:, t, :, :], in_=wds_raw[:, :, t::PACK])
 
         def permute_wd():
+            for t in range(2, PACK):
+                nc.vector.tensor_copy(out=wds[:, t, :, :], in_=wds_raw[:, :, t::PACK])
             for g in range(G):
                 nc.vector.tensor_copy(
                     out=wd[:, g * R : (g + 1) * R].rearrange("p (t m) -> p t m", t=PACK),
@@ -127,16 +129,23 @@ def tile_mla_pa_t_w8_kernel(
         gx = gain_x[:].rearrange("p (j e) -> p j e", e=2)
         nc.gpsimd.tensor_scalar(out=gx[:, :, 0:1], in0=gv[:, :, 1:2], scalar1=-1.0, scalar2=0.0, op0=ALU.mult, op1=ALU.add)
         nc.gpsimd.tensor_copy(out=gx[:, :, 1:2], in_=gv[:, :, 0:1])
-        for tab, trig, w in ((ta, cos_t, gv), (tb, sin_t, gx)):
-            nc.gpsimd.tensor_tensor(
-                out=tab[:].rearrange("p i (j e) -> p i j e", e=2),
-                in0=trig[:].unsqueeze(3).to_broadcast([P, IT, D // 2, 2]),
-                in1=w.unsqueeze(1).to_broadcast([P, IT, D // 2, 2]),
-                op=ALU.mult,
-            )
+
+        def tables(q):
+            c = slice(2 * q, 2 * q + 2)
+            for tab, trig, w in ((ta, cos_t, gv), (tb, sin_t, gx)):
+                nc.gpsimd.tensor_tensor(
+                    out=tab[:, c, :].rearrange("p i (j e) -> p i j e", e=2),
+                    in0=trig[:, c, :].unsqueeze(3).to_broadcast([P, 2, D // 2, 2]),
+                    in1=w.unsqueeze(1).to_broadcast([P, 2, D // 2, 2]),
+                    op=ALU.mult,
+                )
+
+        tables(0)
 
         def turn(n, g):
             xt = psum.tile([P, 2, 2, P], F32, name="xt%d" % g)
+            if n >= 4:
+                dummy(xt[:].rearrange("p u a n -> p (u a n)"))
             for u in range(2):
                 for a in range(2):
                     words = st["xw", n, a][:].bitcast(F32)
@@ -203,6 +212,8 @@ def tile_mla_pa_t_w8_kernel(
         def mm_up(n, a, half):
             lq, lqs = st["lq", n]
             dst = psum.tile([P, HD], F32, name="%s%d" % ("kv"[half], a))
+            if half == 0 and a == 1 and 0 < n:
+                dummy(dst[:])
             c = slice(half * HD, (half + 1) * HD)
             m = slice(a * P, (a + 1) * P)
             nc.tensor.matmul_mx(
@@ -216,10 +227,9 @@ def tile_mla_pa_t_w8_kernel(
             )
             st["kv"[half], n, a] = dst
 
-        def dummy(n):
-            junk = psum.tile([P, HD], F32, name="lat1")
+        def dummy(bank):
             nc.tensor.matmul_mx(
-                out=junk[:],
+                out=bank,
                 lhsT=wd[:, :P].bitcast(FP8X4),
                 lhsT_scale=wds[:, 0, 0, :],
                 rhs=wu[:, :HD].bitcast(FP8X4),
@@ -257,9 +267,12 @@ def tile_mla_pa_t_w8_kernel(
             b, i = divmod(2 * n, IT)
             nc.sync.dma_start(out=out[b].rearrange("(p i) h d -> p i (h d)", i=IT)[:, i : i + 2, :], in_=tile[:])
 
-        H_STT, H_ACT, H_POOL = 0, 0, 4
+        H_STT = 2
 
-        def products(n, a, hs):
+        def stt_heads(n):
+            return H_STT if n < NP - 1 else 0
+
+        def products(n, a, hs, parts="ps"):
             kp = st["k", n, a]
             rstd = st["rstd", n, a]
             if ("t", n, a) not in st:
@@ -268,8 +281,8 @@ def tile_mla_pa_t_w8_kernel(
                 st["t", n, a] = (t1, t2)
             t1, t2 = st["t", n, a]
             i = (2 * n + a) % IT
-            plain = [h for h in hs if h >= H_STT]
-            if plain:
+            plain = [h for h in hs if h >= stt_heads(n)]
+            if plain and "p" in parts:
                 m = len(plain)
                 c = slice(plain[0] * D, (plain[-1] + 1) * D)
                 nc.vector.tensor_tensor(
@@ -285,7 +298,7 @@ def tile_mla_pa_t_w8_kernel(
                     op=ALU.mult,
                 )
             for h in hs:
-                if h >= H_STT:
+                if h >= stt_heads(n) or "s" not in parts:
                     continue
                 c = slice(h * D, (h + 1) * D)
                 nc.vector.scalar_tensor_tensor(
@@ -338,16 +351,12 @@ def tile_mla_pa_t_w8_kernel(
         def ok(n):
             return 0 <= n < NP
 
-        TAIL = 2
-
-        def fin_heads(n, who):
-            act = H if n >= NP - TAIL else H_ACT
-            return range(act) if who == "s" else range(act, H)
-
-        def adder(n, a):
-            return nc.vector if n >= NP - TAIL and a == 1 else nc.gpsimd
+        def s_heads(n):
+            return range(stt_heads(n), H)
 
         for p in range(-5, NP):
+            if ok(p):
+                products(p, 0, range(H), "p")
             if ok(p + 1):
                 quant_l(p + 1)
                 for a in range(2):
@@ -356,23 +365,23 @@ def tile_mla_pa_t_w8_kernel(
             if ok(p):
                 rsqrt(p, 1)
             if ok(p - 1):
-                final(p - 1, 1, fin_heads(p - 1, "s"), "s")
+                final(p - 1, 1, s_heads(p - 1), "s")
+                put(out_k, st["ks", p - 1], p - 1)
             if ok(p + 1):
                 v_out(p + 1, 1)
             if ok(p + 2):
-                quant_x(p + 2)
                 if p + 2 == 0:
                     permute_wd()
+                quant_x(p + 2)
+                if 0 < p + 3 < IT // 2:
+                    tables(p + 3)
                 for a in range(2):
                     mm_down(p + 2, a)
                 for a in range(2):
                     lat_out(p + 2, a)
             if ok(p):
-                products(p, 0, range(H))
-                add(p, 0, adder(p, 0), full)
-            if ok(p - 1):
-                final(p - 1, 1, fin_heads(p - 1, "g"), "g")
-                put(out_k, st["ks", p - 1], p - 1)
+                products(p, 0, range(H), "s")
+                add(p, 0, nc.gpsimd, full)
             if ok(p + 1):
                 mm_up(p + 1, 0, 0)
                 squares(p + 1, 0)
@@ -384,34 +393,27 @@ def tile_mla_pa_t_w8_kernel(
                 cast(p + 5, 1, 0, C, "s")
             if ok(p + 3):
                 scale(p + 3, 0)
-            if ok(p) and ok(p + 1):
-                dummy(p)
             if ok(p + 4):
                 turn(p + 4, 0)
-            if ok(p) and ok(p + 1):
-                dummy(p)
             if ok(p) and p < NP - 1:
                 products(p, 1, range(H))
-                add(p, 1, adder(p, 1), full)
-                final(p, 0, fin_heads(p, "g"), "g")
+                add(p, 1, nc.gpsimd, full)
             elif ok(p):
                 products(p, 1, range(H // 2))
                 add(p, 1, nc.gpsimd, lo)
-                final(p, 0, range(H), "s")
+                final(p, 0, s_heads(p), "s")
                 put_k(p, 0, full)
                 products(p, 1, range(H // 2, H))
                 add(p, 1, nc.vector, hi)
                 final(p, 1, range(H // 2), "s")
                 put_k(p, 1, lo)
-                final(p, 1, range(H // 2, H), "s")
+                final(p, 1, range(H // 2, H), "v")
                 put_k(p, 1, hi)
             if ok(p + 1):
                 mm_up(p + 1, 1, 0)
                 squares(p + 1, 1)
             if ok(p) and p < NP - 1:
-                final(p, 0, fin_heads(p, "s"), "s")
-            if ok(p) and ok(p + 1):
-                dummy(p)
+                final(p, 0, s_heads(p), "s")
             if ok(p + 3):
                 scale(p + 3, 1)
             if ok(p + 4):

from contextlib import ExitStack

import concourse.mybir as mybir
from concourse.masks import make_identity

B, T, C, H, D, R = 4, 1024, 1024, 4, 128, 512
EPS = 1e-6
FLOPS = 2 * B * T * C * R + 2 * B * T * R * 2 * H * D

F32 = mybir.dt.float32
BF16 = mybir.dt.bfloat16
I32 = mybir.dt.int32
U32 = mybir.dt.uint32
U8 = mybir.dt.uint8
FP8 = mybir.dt.float8_e4m3fn
FP8X4 = mybir.dt.float8_e4m3fn_x4
ACT = mybir.ActivationFunctionType
ALU = mybir.AluOpType

P = 128
PACK = 4
IT = T // P
NP = B * IT // 2
HD = H * D
G = C // (P * PACK)


def tile_mla_pa_t_w8_kernel(
    tc, x_bytes, x_scale, wd_words, wd_scales, wu_words, wu_scales, k_norm_w, f_cos, f_sin, out_k, out_v
):
    nc = tc.nc
    with ExitStack() as ctx:
        keep = ctx.enter_context(tc.tile_pool(name="keep", bufs=1))
        work = ctx.enter_context(tc.tile_pool(name="work", bufs=4))
        store = ctx.enter_context(tc.tile_pool(name="store", bufs=4))
        psum = ctx.enter_context(tc.psum_pool(name="psum", bufs=1))
        ctx.enter_context(tc.manual_schedule())

        warm = keep.tile([P, 1], F32, name="warm")
        nc.vector.memset(warm[:], 1.0)
        nc.scalar.activation(out=warm[:], in_=warm[:], func=ACT.Sqrt)

        loads = [(0, 0, 2), (0, 2, 2), (0, 4, 4)]
        loads += [(b, i, 4) for b in range(1, B) for i in (0, 4)]
        bytes_of = {}

        def load_x(entry):
            b, i0, n = entry
            xb = keep.tile([P, n, C], U8, name="xbytes_%d_%d" % (b, i0))
            nc.sync.dma_start(out=xb[:], in_=x_bytes[b].rearrange("(p i) k -> p i k", i=IT)[:, i0 : i0 + n, :])
            for i in range(0, n, 2):
                bytes_of[(b * IT + i0 + i) // 2] = (xb, i)

        load_x(loads[0])
        wds_raw = keep.tile([P, G, R], U8, name="wds_raw", align_bytes=64)
        wus = keep.tile([P, 2 * HD], U8, name="wus", align_bytes=64)
        nc.vector.memset(wds_raw[:].bitcast(I32), 0)
        nc.vector.memset(wus[:].bitcast(I32), 0)
        for q in range(4):
            nc.sync.dma_start(
                out=wds_raw[32 * q : 32 * q + 4, :, :].bitcast(I32),
                in_=wd_scales[:, 4 * q : 4 * q + 4, :].rearrange("g q n -> q g n").bitcast(I32),
            )
        load_x(loads[1])
        wd_raw = keep.tile([P, G * R], I32, name="wd_raw", align_bytes=64)
        for g in range(G):
            nc.sync.dma_start(
                out=wd_raw[:, g * R : (g + 1) * R], in_=wd_words[g].rearrange("p n t -> p (n t)").bitcast(I32)
            )
        load_x(loads[2])
        for q in range(4):
            nc.sync.dma_start(
                out=wus[32 * q : 32 * q + 4, :].bitcast(I32), in_=wu_scales[0, 4 * q : 4 * q + 4, :].bitcast(I32)
            )
        wu = keep.tile([P, 2 * HD], I32, name="wu", align_bytes=64)
        nc.sync.dma_start(out=wu[:], in_=wu_words[0].rearrange("p n t -> p (n t)").bitcast(I32))
        for entry in loads[3:]:
            load_x(entry)

        xs = keep.tile([P, G * PACK], F32, name="xs")
        nc.scalar.dma_start(
            out=xs[:].rearrange("p (g t) -> p g t", t=PACK),
            in_=x_scale.rearrange("a b (g p t) -> p (a b g) t", g=G, t=PACK),
        )
        cos_t = keep.tile([P, IT, D // 2], BF16, name="cos_t")
        sin_t = keep.tile([P, IT, D // 2], BF16, name="sin_t")
        gain = keep.tile([P, D], BF16, name="gain")
        nc.scalar.dma_start(out=cos_t[:], in_=f_cos.rearrange("(p i) j -> p i j", i=IT))
        nc.scalar.dma_start(out=sin_t[:], in_=f_sin.rearrange("(p i) j -> p i j", i=IT))
        nc.scalar.dma_start(out=gain[:], in_=k_norm_w.partition_broadcast(P))

        ident = keep.tile([P, P], F32, name="ident")
        make_identity(nc, ident[:])

        st = {}

        def cast(n, a, lo, hi, eng):
            xb, i = bytes_of[n]
            if ("xw", n, a) not in st:
                st["xw", n, a] = work.tile([P, C], BF16, name="xw%d" % a)
            xw = st["xw", n, a]
            if eng == "v":
                nc.vector.tensor_copy(out=xw[:, lo:hi], in_=xb[:, i + a, lo:hi].bitcast(FP8))
            else:
                nc.scalar.copy(out=xw[:, lo:hi], in_=xb[:, i + a, lo:hi].bitcast(FP8))

        for g in range(G):
            cast(0, 0, g * 512, (g + 1) * 512, "v")
            cast(0, 1, g * 512, (g + 1) * 512, "s")

        wd = keep.tile([P, G * R], I32, name="wd", align_bytes=64)
        wds = keep.tile([P, PACK, G, P], U8, name="wds", align_bytes=64)
        for t in range(2):
            nc.vector.tensor_copy(out=wds[:, t, :, :], in_=wds_raw[:, :, t::PACK])

        def permute_wd():
            for t in range(2, PACK):
                nc.vector.tensor_copy(out=wds[:, t, :, :], in_=wds_raw[:, :, t::PACK])
            for g in range(G):
                nc.vector.tensor_copy(
                    out=wd[:, g * R : (g + 1) * R].rearrange("p (t m) -> p t m", t=PACK),
                    in_=wd_raw[:, g * R : (g + 1) * R].rearrange("p (m t) -> p t m", t=PACK),
                )

        gain_x = keep.tile([P, D], F32, name="gain_x")
        ta = keep.tile([P, IT, D], F32, name="ta")
        tb = keep.tile([P, IT, D], F32, name="tb")
        gv = gain[:].rearrange("p (j e) -> p j e", e=2)
        gx = gain_x[:].rearrange("p (j e) -> p j e", e=2)
        nc.gpsimd.tensor_scalar(out=gx[:, :, 0:1], in0=gv[:, :, 1:2], scalar1=-1.0, scalar2=0.0, op0=ALU.mult, op1=ALU.add)
        nc.gpsimd.tensor_copy(out=gx[:, :, 1:2], in_=gv[:, :, 0:1])

        def tables(q):
            c = slice(2 * q, 2 * q + 2)
            for tab, trig, w in ((ta, cos_t, gv), (tb, sin_t, gx)):
                nc.gpsimd.tensor_tensor(
                    out=tab[:, c, :].rearrange("p i (j e) -> p i j e", e=2),
                    in0=trig[:, c, :].unsqueeze(3).to_broadcast([P, 2, D // 2, 2]),
                    in1=w.unsqueeze(1).to_broadcast([P, 2, D // 2, 2]),
                    op=ALU.mult,
                )

        tables(0)

        def turn(n, g):
            xt = psum.tile([P, 2, 2, P], F32, name="xt%d" % g)
            if n >= 4:
                dummy(xt[:].rearrange("p u a n -> p (u a n)"))
            for u in range(2):
                for a in range(2):
                    words = st["xw", n, a][:].bitcast(F32)
                    nc.tensor.transpose(xt[:, u, a, :], words[:, 256 * g + u : 256 * (g + 1) : 2], ident[:])
            st["xt", n, g] = xt

        def scale(n, g):
            xt = st.pop(("xt", n, g))
            if g == 0:
                st["xg", n] = work.tile([P, G * 1024], BF16, name="xg", align_bytes=64)
            xg = st["xg", n]
            nc.vector.tensor_tensor(
                out=xg[:, g * 1024 : (g + 1) * 1024].rearrange("p (n u e) -> p n u e", u=2, e=2),
                in0=xs[:, g * PACK : (g + 1) * PACK]
                .rearrange("p (u e) -> p u e", e=2)
                .unsqueeze(1)
                .to_broadcast([P, 2 * P, 2, 2]),
                in1=xt[:].rearrange("p u a n -> p (u a n)").bitcast(BF16).rearrange("p (u n e) -> p n u e", u=2, e=2),
                op=ALU.mult,
            )

        def quant_x(n):
            xg = st.pop(("xg", n))
            xq = work.tile([P, G * 2 * P], U32, name="xq", align_bytes=64)
            xqs = work.tile([P, G * 2 * P], U8, name="xqs", align_bytes=64)
            nc.vector.quantize_mx(out=xq[:].bitcast(FP8X4), scales=xqs[:], in_=xg[:])
            st["xq", n] = (xq, xqs)

        def mm_down(n, a):
            xq, xqs = st["xq", n]
            lat = psum.tile([P, PACK * P], F32, name="lat%d" % a)
            for t in range(PACK):
                for g in range(G):
                    c = slice(t * P, (t + 1) * P)
                    m = slice((2 * g + a) * P, (2 * g + a + 1) * P)
                    nc.tensor.matmul_mx(
                        out=lat[:, c],
                        lhsT=wd[:, g * R + t * P : g * R + (t + 1) * P].bitcast(FP8X4),
                        lhsT_scale=wds[:, t, g, :],
                        rhs=xq[:, m].bitcast(FP8X4),
                        rhs_scale=xqs[:, m],
                        start=(g == 0),
                        stop=(g == G - 1),
                    )
            st["lat", n, a] = lat

        def lat_out(n, a):
            lat = st.pop(("lat", n, a))
            if a == 0:
                st["lg", n] = work.tile([P, 2 * PACK * P], BF16, name="lg", align_bytes=64)
            lg = st["lg", n]
            nc.scalar.copy(
                out=lg[:, a * 512 : (a + 1) * 512].rearrange("p (n t) -> p n t", t=PACK),
                in_=lat[:].rearrange("p (t n) -> p n t", t=PACK),
            )

        def quant_l(n):
            lg = st.pop(("lg", n))
            lq = work.tile([P, 2 * P], U32, name="lq", align_bytes=64)
            lqs = work.tile([P, 2 * P], U8, name="lqs", align_bytes=64)
            nc.vector.quantize_mx(out=lq[:].bitcast(FP8X4), scales=lqs[:], in_=lg[:])
            st["lq", n] = (lq, lqs)

        def mm_up(n, a, half):
            lq, lqs = st["lq", n]
            dst = psum.tile([P, HD], F32, name="%s%d" % ("kv"[half], a))
            if half == 0 and a == 1 and 0 < n:
                dummy(dst[:])
            c = slice(half * HD, (half + 1) * HD)
            m = slice(a * P, (a + 1) * P)
            nc.tensor.matmul_mx(
                out=dst[:],
                lhsT=lq[:, m].bitcast(FP8X4),
                lhsT_scale=lqs[:, m],
                rhs=wu[:, c].bitcast(FP8X4),
                rhs_scale=wus[:, c],
                start=True,
                stop=True,
            )
            st["kv"[half], n, a] = dst

        def dummy(bank):
            nc.tensor.matmul_mx(
                out=bank,
                lhsT=wd[:, :P].bitcast(FP8X4),
                lhsT_scale=wds[:, 0, 0, :],
                rhs=wu[:, :HD].bitcast(FP8X4),
                rhs_scale=wus[:, :HD],
                start=True,
                stop=True,
            )

        def squares(n, a):
            kp = st["k", n, a]
            ss = work.tile([P, H], F32, name="ss%d" % a)
            junk = work.tile([P, HD], BF16, name="junk")
            for h in range(H):
                nc.scalar.activation(
                    out=junk[:, h * D : (h + 1) * D], in_=kp[:, h * D : (h + 1) * D], func=ACT.Square, accum_out=ss[:, h : h + 1]
                )
            st["ss", n, a] = ss

        def rsqrt(n, a):
            ss = st.pop(("ss", n, a))
            rstd = work.tile([P, H], F32, name="rstd%d" % a)
            nc.scalar.activation(out=rstd[:], in_=ss[:], func=ACT.Abs_reciprocal_sqrt, scale=1.0 / D, bias=EPS)
            st["rstd", n, a] = rstd

        def v_out(n, a):
            vp = st.pop(("v", n, a))
            if a == 0:
                st["vs"] = store.tile([P, 2, HD], F32, name="vs")
            vs = st["vs"]
            nc.scalar.copy(out=vs[:, a, :], in_=vp[:])
            if a == 1:
                put(out_v, vs, n)

        def put(out, tile, n):
            b, i = divmod(2 * n, IT)
            nc.sync.dma_start(out=out[b].rearrange("(p i) h d -> p i (h d)", i=IT)[:, i : i + 2, :], in_=tile[:])

        H_STT = 2

        def stt_heads(n):
            return H_STT if n < NP - 1 else 0

        def products(n, a, hs, parts="ps"):
            kp = st["k", n, a]
            rstd = st["rstd", n, a]
            if ("t", n, a) not in st:
                t1 = work.tile([P, HD], F32, name="t1")
                t2 = work.tile([P, HD], F32, name="t2")
                st["t", n, a] = (t1, t2)
            t1, t2 = st["t", n, a]
            i = (2 * n + a) % IT
            plain = [h for h in hs if h >= stt_heads(n)]
            if plain and "p" in parts:
                m = len(plain)
                c = slice(plain[0] * D, (plain[-1] + 1) * D)
                nc.vector.tensor_tensor(
                    out=t1[:, c].rearrange("p (h d) -> p h d", d=D),
                    in0=ta[:, i : i + 1, :].to_broadcast([P, m, D]),
                    in1=kp[:, c].rearrange("p (h d) -> p h d", d=D),
                    op=ALU.mult,
                )
                nc.vector.tensor_tensor(
                    out=t2[:, c].rearrange("p (h j e) -> p h j e", j=D // 2, e=2),
                    in0=tb[:, i : i + 1, :].rearrange("p h (j e) -> p h j e", e=2).to_broadcast([P, m, D // 2, 2]),
                    in1=kp[:, c].rearrange("p (h j e) -> p h j e", j=D // 2, e=2)[:, :, :, ::-1],
                    op=ALU.mult,
                )
            for h in hs:
                if h >= stt_heads(n) or "s" not in parts:
                    continue
                c = slice(h * D, (h + 1) * D)
                nc.vector.scalar_tensor_tensor(
                    out=t1[:, c], in0=ta[:, i, :], scalar=rstd[:, h : h + 1], in1=kp[:, c], op0=ALU.mult, op1=ALU.mult
                )
                nc.vector.scalar_tensor_tensor(
                    out=t2[:, c].rearrange("p (j e) -> p j e", e=2),
                    in0=tb[:, i, :].rearrange("p (j e) -> p j e", e=2),
                    scalar=rstd[:, h : h + 1],
                    in1=kp[:, c].rearrange("p (j e) -> p j e", e=2)[:, :, ::-1],
                    op0=ALU.mult,
                    op1=ALU.mult,
                )

        def add(n, a, eng, c):
            t1, t2 = st["t", n, a]
            if ("ks", n) not in st:
                st["ks", n] = store.tile([P, 2, HD], F32, name="ks")
            ks = st["ks", n]
            w = (c.stop - c.start) // 1
            for c0 in range(c.start, c.stop, w):
                eng.tensor_tensor(
                    out=ks[:, a, c0 : c0 + w], in0=t1[:, c0 : c0 + w], in1=t2[:, c0 : c0 + w], op=ALU.add
                )

        def final(n, a, hs, who):
            ks = st["ks", n]
            rstd = st["rstd", n, a]
            for h in hs:
                c = slice(h * D, (h + 1) * D)
                if who == "s":
                    nc.scalar.activation(out=ks[:, a, c], in_=ks[:, a, c], func=ACT.Copy, scale=rstd[:, h : h + 1])
                elif who == "v":
                    nc.vector.tensor_scalar(
                        out=ks[:, a, c], in0=ks[:, a, c], scalar1=rstd[:, h : h + 1], scalar2=None, op0=ALU.mult
                    )
                else:
                    nc.gpsimd.tensor_scalar(
                        out=ks[:, a, c], in0=ks[:, a, c], scalar1=rstd[:, h : h + 1], scalar2=0.0, op0=ALU.mult, op1=ALU.add
                    )

        def put_k(n, a, c):
            ks = st["ks", n]
            b, i = divmod(2 * n + a, IT)
            nc.sync.dma_start(out=out_k[b].rearrange("(p i) h d -> p i (h d)", i=IT)[:, i, c], in_=ks[:, a, c])

        full = slice(0, HD)
        lo, hi = slice(0, HD // 2), slice(HD // 2, HD)

        def ok(n):
            return 0 <= n < NP

        def s_heads(n):
            return range(stt_heads(n), H)

        for p in range(-5, NP):
            if ok(p):
                products(p, 0, range(H), "p")
            if ok(p + 1):
                quant_l(p + 1)
                for a in range(2):
                    mm_up(p + 1, a, 1)
                v_out(p + 1, 0)
            if ok(p):
                rsqrt(p, 1)
            if ok(p - 1):
                final(p - 1, 1, s_heads(p - 1), "s")
                put(out_k, st["ks", p - 1], p - 1)
            if ok(p + 1):
                v_out(p + 1, 1)
            if ok(p + 2):
                if p + 2 == 0:
                    permute_wd()
                quant_x(p + 2)
                if 0 < p + 3 < IT // 2:
                    tables(p + 3)
                for a in range(2):
                    mm_down(p + 2, a)
                for a in range(2):
                    lat_out(p + 2, a)
            if ok(p):
                products(p, 0, range(H), "s")
                add(p, 0, nc.gpsimd, full)
            if ok(p + 1):
                mm_up(p + 1, 0, 0)
                squares(p + 1, 0)
            if 0 < p + 5 < NP:
                cast(p + 5, 0, 0, C, "s")
            if ok(p + 1):
                rsqrt(p + 1, 0)
            if 0 < p + 5 < NP:
                cast(p + 5, 1, 0, C, "s")
            if ok(p + 3):
                scale(p + 3, 0)
            if ok(p + 4):
                turn(p + 4, 0)
            if ok(p) and p < NP - 1:
                products(p, 1, range(H))
                add(p, 1, nc.gpsimd, full)
            elif ok(p):
                products(p, 1, range(H // 2))
                add(p, 1, nc.gpsimd, lo)
                final(p, 0, s_heads(p), "s")
                put_k(p, 0, full)
                products(p, 1, range(H // 2, H))
                add(p, 1, nc.vector, hi)
                final(p, 1, range(H // 2), "s")
                put_k(p, 1, lo)
                final(p, 1, range(H // 2, H), "v")
                put_k(p, 1, hi)
            if ok(p + 1):
                mm_up(p + 1, 1, 0)
                squares(p + 1, 1)
            if ok(p) and p < NP - 1:
                final(p, 0, s_heads(p), "s")
            if ok(p + 3):
                scale(p + 3, 1)
            if ok(p + 4):
                turn(p + 4, 1)
